import numpy as np
import ml_dtypes

BF16 = ml_dtypes.bfloat16


def bf(x):
    return np.asarray(x, np.float32).astype(BF16)


def f32(x):
    return np.asarray(x, np.float32)


def f64(x):
    return np.asarray(x).astype(np.float64)


def striped(idx):
    return np.tile(idx.reshape(-1, 16).T, (8, 1))


H, D, M, S, K, N = 256, 256, 512, 4096, 2, 8192


def setup_inputs():
    return {"hidden": bf(np.random.standard_normal((H, S))), "w": bf(np.random.standard_normal((H, M)) / np.sqrt(H)), "b": f32(0.1 * np.random.standard_normal((M, 1))), "offs": striped(np.concatenate([np.random.permutation(S) for _ in range(K)]))}


def reference(hidden, w, b, offs):
    idx = offs[:16].T.reshape(-1)
    proj = f64(w).T @ f64(hidden) + f64(b)
    q, k = proj[:D], proj[D:]
    prod = k[:, idx] * np.tile(q, (1, K))
    return prod.sum(axis=0).reshape(K, S).sum(axis=0, keepdims=True) / np.sqrt(D)

@@ -1,0 +1,104 @@
+import math
+
+import concourse.mybir as mybir
+
+BF16, F32, U16 = mybir.dt.bfloat16, mybir.dt.float32, mybir.dt.uint16
+MULT = mybir.AluOpType.mult
+IDENTITY = mybir.ActivationFunctionType.Identity
+COPY = mybir.ActivationFunctionType.Copy
+
+P = 128
+H = 256
+D = 256
+S = 4096
+ENDS = 2
+BANK = 512
+LOAD = 1024
+PIECE = 1024
+
+FLOPS = 2 * H * (2 * D) * S + 2 * D * ENDS * S
+
+
+def tile_customrelation_kernel(tc, hidden, w, b, offs, out):
+    nc = tc.nc
+    with (
+        tc.tile_pool(name="held", bufs=1) as held,
+        tc.tile_pool(name="products", bufs=4) as products,
+        tc.psum_pool(name="projected", bufs=6) as projected,
+        tc.psum_pool(name="summed", bufs=1) as summed,
+    ):
+        offsets = held.tile([P, ENDS * S // 16], U16, name="offsets")
+        weights = [held.tile([P, 2 * D], BF16, name=f"weights{h}") for h in range(H // P)]
+        tokens = [held.tile([P, S], BF16, name=f"tokens{h}") for h in range(H // P)]
+        bias = held.tile([P, 2 * D // P], F32, name="bias")
+        queries = [held.tile([P, S], F32, name=f"queries{c}") for c in range(D // P)]
+        keys = [held.tile([P, S], F32, name=f"keys{c}") for c in range(D // P)]
+
+        queues = (nc.sync, nc.scalar)
+        for h in range(H // P):
+            queues[h].dma_start(weights[h][:], w[h * P : (h + 1) * P, :])
+        with nc.allow_non_contiguous_dma(reason="512 biases, one to a partition and column"):
+            nc.gpsimd.dma_start(bias[:], b.rearrange("(g p) o -> p (g o)", p=P))
+        for first in range(0, S, LOAD):
+            for h in range(H // P):
+                queues[h].dma_start(
+                    tokens[h][:, first : first + LOAD], hidden[h * P : (h + 1) * P, first : first + LOAD]
+                )
+        nc.sync.dma_start(offsets[:], offs)
+
+        selector = held.tile([P, (S // BANK) * P], BF16, name="selector")
+        nc.gpsimd.memset(selector[:], 0.0)
+        for r in range(S // BANK):
+            nc.gpsimd.memset(selector[:, r * P + r : r * P + r + 1], 1.0 / math.sqrt(D))
+
+        def project(block, t, rows, on_vector):
+            columns = slice(t * BANK, (t + 1) * BANK)
+            projection = projected.tile([P, BANK], F32, name="projection")
+            for h in range(H // P):
+                nc.tensor.matmul(
+                    projection[:],
+                    weights[h][:, block * P : (block + 1) * P],
+                    tokens[h][:, columns],
+                    start=(h == 0),
+                    stop=(h == H // P - 1),
+                )
+            if on_vector:
+                nc.vector.tensor_scalar_add(rows[:, columns], projection[:], bias[:, block : block + 1])
+            else:
+                nc.scalar.activation(rows[:, columns], projection[:], IDENTITY, bias=bias[:, block : block + 1])
+
+        for t in range(S // BANK):
+            project(D // P, t, keys[0], on_vector=(t % 2 == 1))
+
+        scores = summed.tile([P, BANK], F32, name="scores")
+        for c in range(D // P):
+            for first in range(0, S, PIECE):
+                banks = range(first // BANK, (first + PIECE) // BANK)
+                for t in banks:
+                    project(c, t, queries[c], on_vector=False)
+                if c + 1 < D // P:
+                    for t in banks:
+                        project(D // P + c + 1, t, keys[c + 1], on_vector=False)
+                for e in range(ENDS):
+                    entry = (e * S + first) // 16
+                    product = products.tile([P, PIECE], F32, name="product")
+                    nc.vector.tensor_tensor(
+                        product[:],
+                        keys[c][:].indirect(offsets[:, entry : entry + PIECE // 16]),
+                        queries[c][:, first : first + PIECE],
+                        MULT,
+                    )
+                    rounded = products.tile([P, PIECE], BF16, name="rounded")
+                    nc.scalar.activation(rounded[:], product[:], COPY)
+                    for t in banks:
+                        nc.tensor.matmul(
+                            scores[:],
+                            selector[:, t * P : (t + 1) * P],
+                            rounded[:, t * BANK - first : (t + 1) * BANK - first],
+                            start=(c == 0 and e == 0 and t == 0),
+                            stop=(c == D // P - 1 and e == ENDS - 1 and t == S // BANK - 1),
+                        )
+
+        result = held.tile([S // BANK, BANK], F32, name="result")
+        nc.scalar.activation(result[:], scores[: S // BANK, :], COPY)
+        nc.sync.dma_start(out.rearrange("o (r n) -> (o r) n", n=BANK), result[:])

@@ -13,8 +13,9 @@ D = 256
 S = 4096
 ENDS = 2
 BANK = 512
-LOAD = 1024
-PIECE = 1024
+LOAD = 512
+GROUPS = (512, 512, 1024, 1024, 1024)
+WARMUP = 4
 
 FLOPS = 2 * H * (2 * D) * S + 2 * D * ENDS * S
 
@@ -23,28 +24,32 @@ def tile_customrelation_kernel(tc, hidden, w, b, offs, out):
     nc = tc.nc
     with (
         tc.tile_pool(name="held", bufs=1) as held,
-        tc.tile_pool(name="products", bufs=4) as products,
+        tc.tile_pool(name="products", bufs=10) as products,
+        tc.tile_pool(name="roundeds", bufs=4) as roundeds,
         tc.psum_pool(name="projected", bufs=6) as projected,
         tc.psum_pool(name="summed", bufs=1) as summed,
     ):
         offsets = held.tile([P, ENDS * S // 16], U16, name="offsets")
-        weights = [held.tile([P, 2 * D], BF16, name=f"weights{h}") for h in range(H // P)]
-        tokens = [held.tile([P, S], BF16, name=f"tokens{h}") for h in range(H // P)]
+        weights = held.tile([P, H // P, 2 * D], BF16, name="weights")
+        tokens = held.tile([P, H // P, S], BF16, name="tokens")
         bias = held.tile([P, 2 * D // P], F32, name="bias")
         queries = [held.tile([P, S], F32, name=f"queries{c}") for c in range(D // P)]
         keys = [held.tile([P, S], F32, name=f"keys{c}") for c in range(D // P)]
 
-        queues = (nc.sync, nc.scalar)
-        for h in range(H // P):
-            queues[h].dma_start(weights[h][:], w[h * P : (h + 1) * P, :])
+        nc.sync.dma_start(weights[:], w.rearrange("(h p) m -> p h m", p=P))
         with nc.allow_non_contiguous_dma(reason="512 biases, one to a partition and column"):
-            nc.gpsimd.dma_start(bias[:], b.rearrange("(g p) o -> p (g o)", p=P))
-        for first in range(0, S, LOAD):
-            for h in range(H // P):
-                queues[h].dma_start(
-                    tokens[h][:, first : first + LOAD], hidden[h * P : (h + 1) * P, first : first + LOAD]
-                )
+            nc.scalar.dma_start(bias[:], b.rearrange("(g p) o -> p (g o)", p=P))
+        hidden_blocks = hidden.rearrange("(h p) t -> p h t", p=P)
+        for g in range(S // LOAD):
+            columns = slice(g * LOAD, (g + 1) * LOAD)
+            nc.sync.dma_start(tokens[:, :, columns], hidden_blocks[:, :, columns])
         nc.sync.dma_start(offsets[:], offs)
+
+        zeros = held.tile([P, BANK], BF16, name="zeros")
+        nc.gpsimd.memset(zeros[:], 0.0)
+        unused = summed.tile([P, BANK], F32, name="unused")
+        for i in range(WARMUP):
+            nc.tensor.matmul(unused[:], zeros[:, :P], zeros[:], start=True, stop=True)
 
         selector = held.tile([P, (S // BANK) * P], BF16, name="selector")
         nc.gpsimd.memset(selector[:], 0.0)
@@ -57,8 +62,8 @@ def tile_customrelation_kernel(tc, hidden, w, b, offs, out):
             for h in range(H // P):
                 nc.tensor.matmul(
                     projection[:],
-                    weights[h][:, block * P : (block + 1) * P],
-                    tokens[h][:, columns],
+                    weights[:, h, block * P : (block + 1) * P],
+                    tokens[:, h, columns],
                     start=(h == 0),
                     stop=(h == H // P - 1),
                 )
@@ -69,26 +74,28 @@ def tile_customrelation_kernel(tc, hidden, w, b, offs, out):
 
         for t in range(S // BANK):
             project(D // P, t, keys[0], on_vector=(t % 2 == 1))
+        for t in range(S // BANK):
+            project(0, t, queries[0], on_vector=False)
+        for t in range(S // BANK):
+            project(D // P + 1, t, keys[1], on_vector=False)
+        for t in range(S // BANK):
+            project(1, t, queries[1], on_vector=False)
 
         scores = summed.tile([P, BANK], F32, name="scores")
         for c in range(D // P):
-            for first in range(0, S, PIECE):
-                banks = range(first // BANK, (first + PIECE) // BANK)
-                for t in banks:
-                    project(c, t, queries[c], on_vector=False)
-                if c + 1 < D // P:
-                    for t in banks:
-                        project(D // P + c + 1, t, keys[c + 1], on_vector=False)
+            first = 0
+            for width in GROUPS if c == 0 else reversed(GROUPS):
+                banks = range(first // BANK, (first + width) // BANK)
                 for e in range(ENDS):
                     entry = (e * S + first) // 16
-                    product = products.tile([P, PIECE], F32, name="product")
+                    product = products.tile([P, width], F32, name="product")
                     nc.vector.tensor_tensor(
                         product[:],
-                        keys[c][:].indirect(offsets[:, entry : entry + PIECE // 16]),
-                        queries[c][:, first : first + PIECE],
+                        keys[c][:].indirect(offsets[:, entry : entry + width // 16]),
+                        queries[c][:, first : first + width],
                         MULT,
                     )
-                    rounded = products.tile([P, PIECE], BF16, name="rounded")
+                    rounded = roundeds.tile([P, width], BF16, name="rounded")
                     nc.scalar.activation(rounded[:], product[:], COPY)
                     for t in banks:
                         nc.tensor.matmul(
@@ -98,6 +105,7 @@ def tile_customrelation_kernel(tc, hidden, w, b, offs, out):
                             start=(c == 0 and e == 0 and t == 0),
                             stop=(c == D // P - 1 and e == ENDS - 1 and t == S // BANK - 1),
                         )
+                first += width
 
         result = held.tile([S // BANK, BANK], F32, name="result")
         nc.scalar.activation(result[:], scores[: S // BANK, :], COPY)

@@ -14,7 +14,8 @@ S = 4096
 ENDS = 2
 BANK = 512
 LOAD = 512
-GROUPS = (512, 512, 1024, 1024, 1024)
+ROW = 128
+GROUPS = ((512, 512, 1024, 1024, 1024), (1024, 1024, 1024, 512, 256, 128, 128))
 WARMUP = 4
 
 FLOPS = 2 * H * (2 * D) * S + 2 * D * ENDS * S
@@ -51,10 +52,10 @@ def tile_customrelation_kernel(tc, hidden, w, b, offs, out):
         for i in range(WARMUP):
             nc.tensor.matmul(unused[:], zeros[:, :P], zeros[:], start=True, stop=True)
 
-        selector = held.tile([P, (S // BANK) * P], BF16, name="selector")
+        marked = S // ROW - 1
+        selector = held.tile([P, marked + P], BF16, name="selector")
         nc.gpsimd.memset(selector[:], 0.0)
-        for r in range(S // BANK):
-            nc.gpsimd.memset(selector[:, r * P + r : r * P + r + 1], 1.0 / math.sqrt(D))
+        nc.gpsimd.memset(selector[:, marked : marked + 1], 1.0 / math.sqrt(D))
 
         def project(block, t, rows, on_vector):
             columns = slice(t * BANK, (t + 1) * BANK)
@@ -81,11 +82,10 @@ def tile_customrelation_kernel(tc, hidden, w, b, offs, out):
         for t in range(S // BANK):
             project(1, t, queries[1], on_vector=False)
 
-        scores = summed.tile([P, BANK], F32, name="scores")
+        scores = summed.tile([P, ROW], F32, name="scores")
         for c in range(D // P):
             first = 0
-            for width in GROUPS if c == 0 else reversed(GROUPS):
-                banks = range(first // BANK, (first + width) // BANK)
+            for width in GROUPS[c]:
                 for e in range(ENDS):
                     entry = (e * S + first) // 16
                     product = products.tile([P, width], F32, name="product")
@@ -97,16 +97,17 @@ def tile_customrelation_kernel(tc, hidden, w, b, offs, out):
                     )
                     rounded = roundeds.tile([P, width], BF16, name="rounded")
                     nc.scalar.activation(rounded[:], product[:], COPY)
-                    for t in banks:
+                    for token in range(first, first + width, ROW):
+                        r = token // ROW
                         nc.tensor.matmul(
                             scores[:],
-                            selector[:, t * P : (t + 1) * P],
-                            rounded[:, t * BANK - first : (t + 1) * BANK - first],
-                            start=(c == 0 and e == 0 and t == 0),
-                            stop=(c == D // P - 1 and e == ENDS - 1 and t == S // BANK - 1),
+                            selector[:, marked - r : marked - r + P],
+                            rounded[:, token - first : token - first + ROW],
+                            start=(c == 0 and e == 0 and token == 0),
+                            stop=(c == D // P - 1 and e == ENDS - 1 and token + ROW == S),
                         )
                 first += width
 
-        result = held.tile([S // BANK, BANK], F32, name="result")
-        nc.scalar.activation(result[:], scores[: S // BANK, :], COPY)
-        nc.sync.dma_start(out.rearrange("o (r n) -> (o r) n", n=BANK), result[:])
+        result = held.tile([S // ROW, ROW], F32, name="result")
+        nc.vector.tensor_copy(result[:], scores[: S // ROW, :])
+        nc.sync.dma_start(out.rearrange("o (r n) -> (o r) n", n=ROW), result[:])

@@ -13,7 +13,7 @@ D = 256
 S = 4096
 ENDS = 2
 BANK = 512
-LOAD = 512
+LOAD = 1024
 ROW = 128
 GROUPS = ((512, 512, 1024, 1024, 1024), (1024, 1024, 1024, 512, 256, 128, 128))
 WARMUP = 4
@@ -43,7 +43,8 @@ def tile_customrelation_kernel(tc, hidden, w, b, offs, out):
         hidden_blocks = hidden.rearrange("(h p) t -> p h t", p=P)
         for g in range(S // LOAD):
             columns = slice(g * LOAD, (g + 1) * LOAD)
-            nc.sync.dma_start(tokens[:, :, columns], hidden_blocks[:, :, columns])
+            for h in range(H // P):
+                nc.sync.dma_start(tokens[:, h, columns], hidden_blocks[:, h, columns])
         nc.sync.dma_start(offsets[:], offs)
 
         zeros = held.tile([P, BANK], BF16, name="zeros")
@@ -57,30 +58,31 @@ def tile_customrelation_kernel(tc, hidden, w, b, offs, out):
         nc.gpsimd.memset(selector[:], 0.0)
         nc.gpsimd.memset(selector[:, marked : marked + 1], 1.0 / math.sqrt(D))
 
-        def project(block, t, rows, on_vector):
-            columns = slice(t * BANK, (t + 1) * BANK)
-            projection = projected.tile([P, BANK], F32, name="projection")
+        def project(block, banks, rows, vector_helps):
+            projections = {t: projected.tile([P, BANK], F32, name="projection") for t in banks}
             for h in range(H // P):
-                nc.tensor.matmul(
-                    projection[:],
-                    weights[:, h, block * P : (block + 1) * P],
-                    tokens[:, h, columns],
-                    start=(h == 0),
-                    stop=(h == H // P - 1),
-                )
-            if on_vector:
-                nc.vector.tensor_scalar_add(rows[:, columns], projection[:], bias[:, block : block + 1])
-            else:
-                nc.scalar.activation(rows[:, columns], projection[:], IDENTITY, bias=bias[:, block : block + 1])
+                for t in banks:
+                    nc.tensor.matmul(
+                        projections[t][:],
+                        weights[:, h, block * P : (block + 1) * P],
+                        tokens[:, h, t * BANK : (t + 1) * BANK],
+                        start=(h == 0),
+                        stop=(h == H // P - 1),
+                    )
+            for t in banks:
+                columns = slice(t * BANK, (t + 1) * BANK)
+                if vector_helps and t % 2 == 1:
+                    nc.vector.tensor_scalar_add(rows[:, columns], projections[t][:], bias[:, block : block + 1])
+                else:
+                    nc.scalar.activation(
+                        rows[:, columns], projections[t][:], IDENTITY, bias=bias[:, block : block + 1]
+                    )
 
-        for t in range(S // BANK):
-            project(D // P, t, keys[0], on_vector=(t % 2 == 1))
-        for t in range(S // BANK):
-            project(0, t, queries[0], on_vector=False)
-        for t in range(S // BANK):
-            project(D // P + 1, t, keys[1], on_vector=False)
-        for t in range(S // BANK):
-            project(1, t, queries[1], on_vector=False)
+        for g in range(S // LOAD):
+            project(D // P, range(g * LOAD // BANK, (g + 1) * LOAD // BANK), keys[0], vector_helps=True)
+        for block, rows in ((0, queries[0]), (D // P + 1, keys[1]), (1, queries[1])):
+            for t in range(S // BANK):
+                project(block, (t,), rows, vector_helps=False)
 
         scores = summed.tile([P, ROW], F32, name="scores")
         for c in range(D // P):

@@ -33,19 +33,27 @@ def tile_customrelation_kernel(tc, hidden, w, b, offs, out):
         offsets = held.tile([P, ENDS * S // 16], U16, name="offsets")
         weights = held.tile([P, H // P, 2 * D], BF16, name="weights")
         tokens = held.tile([P, H // P, S], BF16, name="tokens")
-        bias = held.tile([P, 2 * D // P], F32, name="bias")
+        biases = [held.tile([P, 1], F32, name=f"bias{block}") for block in range(2 * D // P)]
         queries = [held.tile([P, S], F32, name=f"queries{c}") for c in range(D // P)]
         keys = [held.tile([P, S], F32, name=f"keys{c}") for c in range(D // P)]
 
-        nc.sync.dma_start(weights[:], w.rearrange("(h p) m -> p h m", p=P))
-        with nc.allow_non_contiguous_dma(reason="512 biases, one to a partition and column"):
-            nc.scalar.dma_start(bias[:], b.rearrange("(g p) o -> p (g o)", p=P))
+        w_blocks = w.rearrange("(h p) m -> p h m", p=P)
+
+        def load_block(block):
+            members = slice(block * P, (block + 1) * P)
+            nc.sync.dma_start(weights[:, :, members], w_blocks[:, :, members])
+            nc.sync.dma_start(biases[block][:], b[members, :])
+
+        load_block(D // P)
         hidden_blocks = hidden.rearrange("(h p) t -> p h t", p=P)
         for g in range(S // LOAD):
             columns = slice(g * LOAD, (g + 1) * LOAD)
             for h in range(H // P):
                 nc.sync.dma_start(tokens[:, h, columns], hidden_blocks[:, h, columns])
+        load_block(0)
         nc.sync.dma_start(offsets[:], offs)
+        load_block(D // P + 1)
+        load_block(1)
 
         zeros = held.tile([P, BANK], BF16, name="zeros")
         nc.gpsimd.memset(zeros[:], 0.0)
@@ -72,10 +80,10 @@ def tile_customrelation_kernel(tc, hidden, w, b, offs, out):
             for t in banks:
                 columns = slice(t * BANK, (t + 1) * BANK)
                 if vector_helps and t % 2 == 1:
-                    nc.vector.tensor_scalar_add(rows[:, columns], projections[t][:], bias[:, block : block + 1])
+                    nc.vector.tensor_scalar_add(rows[:, columns], projections[t][:], biases[block][:])
                 else:
                     nc.scalar.activation(
-                        rows[:, columns], projections[t][:], IDENTITY, bias=bias[:, block : block + 1]
+                        rows[:, columns], projections[t][:], IDENTITY, bias=biases[block][:]
                     )
 
         for g in range(S // LOAD):

@@ -15,10 +15,19 @@ ENDS = 2
 BANK = 512
 LOAD = 1024
 ROW = 128
-GROUPS = ((512, 512, 1024, 1024, 1024), (1024, 1024, 1024, 512, 256, 128, 128))
+GROUPS = ((256, 256, 512, 1024, 1024, 1024), (1024, 1024, 1024, 512, 256, 128, 128))
 WARMUP = 4
 
 FLOPS = 2 * H * (2 * D) * S + 2 * D * ENDS * S
+
+
+def cut(widths, most, first=0):
+    pieces = []
+    for width in widths:
+        step = min(width, most)
+        pieces.extend([(start, step) for start in range(first, first + width, step)])
+        first += width
+    return pieces
 
 
 def tile_customrelation_kernel(tc, hidden, w, b, offs, out):
@@ -46,10 +55,11 @@ def tile_customrelation_kernel(tc, hidden, w, b, offs, out):
 
         load_block(D // P)
         hidden_blocks = hidden.rearrange("(h p) t -> p h t", p=P)
-        for g in range(S // LOAD):
-            columns = slice(g * LOAD, (g + 1) * LOAD)
+        for group, width in cut((S,), LOAD):
             for h in range(H // P):
-                nc.sync.dma_start(tokens[:, h, columns], hidden_blocks[:, h, columns])
+                is_last = group + width == S and h == H // P - 1
+                for first, step in cut((width,), BANK if is_last else LOAD, group):
+                    nc.sync.dma_start(tokens[:, h, first : first + step], hidden_blocks[:, h, first : first + step])
         load_block(0)
         nc.sync.dma_start(offsets[:], offs)
         load_block(D // P + 1)
@@ -66,36 +76,36 @@ def tile_customrelation_kernel(tc, hidden, w, b, offs, out):
         nc.gpsimd.memset(selector[:], 0.0)
         nc.gpsimd.memset(selector[:, marked : marked + 1], 1.0 / math.sqrt(D))
 
-        def project(block, banks, rows, vector_helps):
-            projections = {t: projected.tile([P, BANK], F32, name="projection") for t in banks}
+        def project(block, pieces, rows, vector_helps):
+            projections = [projected.tile([P, width], F32, name="projection") for first, width in pieces]
             for h in range(H // P):
-                for t in banks:
+                for (first, width), projection in zip(pieces, projections):
                     nc.tensor.matmul(
-                        projections[t][:],
+                        projection[:],
                         weights[:, h, block * P : (block + 1) * P],
-                        tokens[:, h, t * BANK : (t + 1) * BANK],
+                        tokens[:, h, first : first + width],
                         start=(h == 0),
                         stop=(h == H // P - 1),
                     )
-            for t in banks:
-                columns = slice(t * BANK, (t + 1) * BANK)
-                if vector_helps and t % 2 == 1:
-                    nc.vector.tensor_scalar_add(rows[:, columns], projections[t][:], biases[block][:])
+            for i, ((first, width), projection) in enumerate(zip(pieces, projections)):
+                if vector_helps and i % 2 == 1:
+                    nc.vector.tensor_scalar_add(rows[:, first : first + width], projection[:], biases[block][:])
                 else:
                     nc.scalar.activation(
-                        rows[:, columns], projections[t][:], IDENTITY, bias=biases[block][:]
+                        rows[:, first : first + width], projection[:], IDENTITY, bias=biases[block][:]
                     )
 
-        for g in range(S // LOAD):
-            project(D // P, range(g * LOAD // BANK, (g + 1) * LOAD // BANK), keys[0], vector_helps=True)
-        for block, rows in ((0, queries[0]), (D // P + 1, keys[1]), (1, queries[1])):
-            for t in range(S // BANK):
-                project(block, (t,), rows, vector_helps=False)
+        for group, width in cut((S,), LOAD):
+            project(D // P, cut((width,), BANK, group), keys[0], vector_helps=True)
+        for piece in cut(GROUPS[0], BANK):
+            project(0, [piece], queries[0], vector_helps=False)
+        for block, rows in ((D // P + 1, keys[1]), (1, queries[1])):
+            for piece in cut((S,), BANK):
+                project(block, [piece], rows, vector_helps=False)
 
         scores = summed.tile([P, ROW], F32, name="scores")
         for c in range(D // P):
-            first = 0
-            for width in GROUPS[c]:
+            for first, width in cut(GROUPS[c], S):
                 for e in range(ENDS):
                     entry = (e * S + first) // 16
                     product = products.tile([P, width], F32, name="product")
@@ -116,7 +126,6 @@ def tile_customrelation_kernel(tc, hidden, w, b, offs, out):
                             start=(c == 0 and e == 0 and token == 0),
                             stop=(c == D // P - 1 and e == ENDS - 1 and token + ROW == S),
                         )
-                first += width
 
         result = held.tile([S // ROW, ROW], F32, name="result")
         nc.vector.tensor_copy(result[:], scores[: S // ROW, :])

@@ -15,7 +15,7 @@ ENDS = 2
 BANK = 512
 LOAD = 1024
 ROW = 128
-GROUPS = ((256, 256, 512, 1024, 1024, 1024), (1024, 1024, 1024, 512, 256, 128, 128))
+GROUPS = ((256, 256, 512, 1024, 2048), (2048, 1024, 512, 256, 128, 128))
 WARMUP = 4
 
 FLOPS = 2 * H * (2 * D) * S + 2 * D * ENDS * S
@@ -34,7 +34,7 @@ def tile_customrelation_kernel(tc, hidden, w, b, offs, out):
     nc = tc.nc
     with (
         tc.tile_pool(name="held", bufs=1) as held,
-        tc.tile_pool(name="products", bufs=10) as products,
+        tc.tile_pool(name="products", bufs=12) as products,
         tc.tile_pool(name="roundeds", bufs=4) as roundeds,
         tc.psum_pool(name="projected", bufs=6) as projected,
         tc.psum_pool(name="summed", bufs=1) as summed,

@@ -16,7 +16,7 @@ BANK = 512
 LOAD = 1024
 ROW = 128
 GROUPS = ((256, 256, 512, 1024, 2048), (2048, 1024, 512, 256, 128, 128))
-WARMUP = 4
+WARMUP = 3
 
 FLOPS = 2 * H * (2 * D) * S + 2 * D * ENDS * S
 
@@ -57,8 +57,9 @@ def tile_customrelation_kernel(tc, hidden, w, b, offs, out):
         hidden_blocks = hidden.rearrange("(h p) t -> p h t", p=P)
         for group, width in cut((S,), LOAD):
             for h in range(H // P):
+                is_first = group == 0 and h == 0
                 is_last = group + width == S and h == H // P - 1
-                for first, step in cut((width,), BANK if is_last else LOAD, group):
+                for first, step in cut((width,), BANK if is_first or is_last else LOAD, group):
                     nc.sync.dma_start(tokens[:, h, first : first + step], hidden_blocks[:, h, first : first + step])
         load_block(0)
         nc.sync.dma_start(offsets[:], offs)

import math

import concourse.mybir as mybir

BF16, F32, U16 = mybir.dt.bfloat16, mybir.dt.float32, mybir.dt.uint16
MULT = mybir.AluOpType.mult
IDENTITY = mybir.ActivationFunctionType.Identity
COPY = mybir.ActivationFunctionType.Copy

P = 128
H = 256
D = 256
S = 4096
ENDS = 2
BANK = 512
LOAD = 1024
ROW = 128
GROUPS = ((256, 256, 512, 1024, 2048), (2048, 1024, 512, 256, 128, 128))
WARMUP = 3

FLOPS = 2 * H * (2 * D) * S + 2 * D * ENDS * S


def cut(widths, most, first=0):
    pieces = []
    for width in widths:
        step = min(width, most)
        pieces.extend([(start, step) for start in range(first, first + width, step)])
        first += width
    return pieces


def tile_customrelation_kernel(tc, hidden, w, b, offs, out):
    nc = tc.nc
    with (
        tc.tile_pool(name="held", bufs=1) as held,
        tc.tile_pool(name="products", bufs=12) as products,
        tc.tile_pool(name="roundeds", bufs=4) as roundeds,
        tc.psum_pool(name="projected", bufs=6) as projected,
        tc.psum_pool(name="summed", bufs=1) as summed,
    ):
        offsets = held.tile([P, ENDS * S // 16], U16, name="offsets")
        weights = held.tile([P, H // P, 2 * D], BF16, name="weights")
        tokens = held.tile([P, H // P, S], BF16, name="tokens")
        biases = [held.tile([P, 1], F32, name=f"bias{block}") for block in range(2 * D // P)]
        queries = [held.tile([P, S], F32, name=f"queries{c}") for c in range(D // P)]
        keys = [held.tile([P, S], F32, name=f"keys{c}") for c in range(D // P)]

        w_blocks = w.rearrange("(h p) m -> p h m", p=P)

        def load_block(block):
            members = slice(block * P, (block + 1) * P)
            nc.sync.dma_start(weights[:, :, members], w_blocks[:, :, members])
            nc.sync.dma_start(biases[block][:], b[members, :])

        load_block(D // P)
        hidden_blocks = hidden.rearrange("(h p) t -> p h t", p=P)
        for group, width in cut((S,), LOAD):
            for h in range(H // P):
                is_first = group == 0 and h == 0
                is_last = group + width == S and h == H // P - 1
                for first, step in cut((width,), BANK if is_first or is_last else LOAD, group):
                    nc.sync.dma_start(tokens[:, h, first : first + step], hidden_blocks[:, h, first : first + step])
        load_block(0)
        nc.sync.dma_start(offsets[:], offs)
        load_block(D // P + 1)
        load_block(1)

        zeros = held.tile([P, BANK], BF16, name="zeros")
        nc.gpsimd.memset(zeros[:], 0.0)
        unused = summed.tile([P, BANK], F32, name="unused")
        for i in range(WARMUP):
            nc.tensor.matmul(unused[:], zeros[:, :P], zeros[:], start=True, stop=True)

        marked = S // ROW - 1
        selector = held.tile([P, marked + P], BF16, name="selector")
        nc.gpsimd.memset(selector[:], 0.0)
        nc.gpsimd.memset(selector[:, marked : marked + 1], 1.0 / math.sqrt(D))

        def project(block, pieces, rows, vector_helps):
            projections = [projected.tile([P, width], F32, name="projection") for first, width in pieces]
            for h in range(H // P):
                for (first, width), projection in zip(pieces, projections):
                    nc.tensor.matmul(
                        projection[:],
                        weights[:, h, block * P : (block + 1) * P],
                        tokens[:, h, first : first + width],
                        start=(h == 0),
                        stop=(h == H // P - 1),
                    )
            for i, ((first, width), projection) in enumerate(zip(pieces, projections)):
                if vector_helps and i % 2 == 1:
                    nc.vector.tensor_scalar_add(rows[:, first : first + width], projection[:], biases[block][:])
                else:
                    nc.scalar.activation(
                        rows[:, first : first + width], projection[:], IDENTITY, bias=biases[block][:]
                    )

        for group, width in cut((S,), LOAD):
            project(D // P, cut((width,), BANK, group), keys[0], vector_helps=True)
        for piece in cut(GROUPS[0], BANK):
            project(0, [piece], queries[0], vector_helps=False)
        for block, rows in ((D // P + 1, keys[1]), (1, queries[1])):
            for piece in cut((S,), BANK):
                project(block, [piece], rows, vector_helps=False)

        scores = summed.tile([P, ROW], F32, name="scores")
        for c in range(D // P):
            for first, width in cut(GROUPS[c], S):
                for e in range(ENDS):
                    entry = (e * S + first) // 16
                    product = products.tile([P, width], F32, name="product")
                    nc.vector.tensor_tensor(
                        product[:],
                        keys[c][:].indirect(offsets[:, entry : entry + width // 16]),
                        queries[c][:, first : first + width],
                        MULT,
                    )
                    rounded = roundeds.tile([P, width], BF16, name="rounded")
                    nc.scalar.activation(rounded[:], product[:], COPY)
                    for token in range(first, first + width, ROW):
                        r = token // ROW
                        nc.tensor.matmul(
                            scores[:],
                            selector[:, marked - r : marked - r + P],
                            rounded[:, token - first : token - first + ROW],
                            start=(c == 0 and e == 0 and token == 0),
                            stop=(c == D // P - 1 and e == ENDS - 1 and token + ROW == S),
                        )

        result = held.tile([S // ROW, ROW], F32, name="result")
        nc.vector.tensor_copy(result[:], scores[: S // ROW, :])
        nc.sync.dma_start(out.rearrange("o (r n) -> (o r) n", n=ROW), result[:])
